import numpy as np
import ml_dtypes


def mxq(x, axis, fmt="e4m3"):
    dtype, down = {"e4m3": (ml_dtypes.float8_e4m3fn, 7), "e5m2": (ml_dtypes.float8_e5m2, 14)}[fmt]
    v = np.moveaxis(np.asarray(x, np.float32).astype(ml_dtypes.bfloat16).astype(np.float64), axis, -1)
    blocks = v.reshape(v.shape[:-1] + (-1, 32))
    amax = np.abs(blocks).max(-1, keepdims=True)
    byte = np.maximum(np.where(amax > 0, np.frexp(amax)[1] - 1 + 127, 0) - down, 1)
    scale = np.exp2(byte - 127.0)
    codes = (blocks / scale).astype(np.float32).astype(dtype).astype(np.float64)
    return np.moveaxis((codes * scale).reshape(v.shape), -1, axis)


WIDE = False


def mx_kscale(k):
    if not WIDE:
        return np.ones(k)
    levels = np.array([10, -10, 5, -5, 0])
    a = np.random.permutation(np.resize(levels, k // 512 * 4)).reshape(k // 512, 4)
    idx = np.arange(k)
    return np.exp2(a[idx // 512, idx % 128 // 32])


BF16 = ml_dtypes.bfloat16


def bf(x):
    return np.asarray(x, np.float32).astype(BF16)


def f64(x):
    return np.asarray(x).astype(np.float64)


B, E, D1, D2, WS1, WS2, H, HID = 2, 1024, 32, 16, 8, 8, 32, 2048
NW = (D1 // WS1) * (D2 // WS2)
S = WS1 * WS2
DH = E // H
EPS = 1e-5


def layernorm(v, g, b):
    mu = v.mean(-1, keepdims=True)
    var = v.var(-1, keepdims=True)
    return (v - mu) / np.sqrt(var + EPS) * g + b


def heads(t):
    return t.reshape(B, NW, S, H, DH).transpose(0, 1, 3, 2, 4)


def setup_inputs():
    n = np.random.standard_normal
    s = mx_kscale(E)
    c = 1.0 / np.sqrt(E)
    return {"x": bf(n((B, E, D1, D2))),
            "ln1_g": bf((1.0 + 0.1 * n(E)) * s), "ln1_b": bf(0.1 * n(E) * s),
            "Wq": bf(n((E, E)) * c / s[:, None]), "bq": bf(0.1 * n(E)),
            "Wk": bf(n((E, E)) * c / s[:, None]), "bk": bf(0.1 * n(E)),
            "Wv": bf(n((E, E)) * c / s[:, None]), "bv": bf(0.1 * n(E))}


def reference(x, ln1_g, ln1_b, Wq, bq, Wk, bk, Wv, bv):
    xt = f64(x).transpose(0, 2, 3, 1)
    xn = layernorm(xt, f64(ln1_g), f64(ln1_b))
    xn = np.roll(xn, (-WS1 // 2, -WS2 // 2), axis=(1, 2))
    xw = xn.reshape(B, D1 // WS1, WS1, D2 // WS2, WS2, E).transpose(0, 1, 3, 2, 4, 5).reshape(B, NW, S, E)
    xq = mxq(xw, 3, "e4m3")
    q = ((xq @ mxq(f64(Wq), 0, "e4m3")) + f64(bq)) * DH ** -0.5
    k = (xq @ mxq(f64(Wk), 0, "e4m3")) + f64(bk)
    v = (xq @ mxq(f64(Wv), 0, "e4m3")) + f64(bv)
    return heads(q), heads(k), heads(v)

@@ -1,0 +1,262 @@
+from concourse.masks import make_identity
+import concourse.mybir as mybir
+
+BF16 = mybir.dt.bfloat16
+F32 = mybir.dt.float32
+U32 = mybir.dt.uint32
+U8 = mybir.dt.uint8
+FP8X4 = mybir.dt.float8_e4m3fn_x4
+ACT = mybir.ActivationFunctionType
+ALU = mybir.AluOpType
+
+P = 128
+PACK = 4
+K_PASS = P * PACK
+IMAGES = 2
+E = 1024
+ROWS, COLS = 32, 16
+TOKENS = ROWS * COLS
+WIN = 8
+SHIFT = WIN // 2
+HEAD = 32
+EPS = 1e-5
+PASSES = E // K_PASS
+SLICES = PASSES * PACK
+BLOCK = WIN * COLS
+BANDS = ROWS // WIN
+RUN = (COLS // WIN) * WIN
+N_TILE = 512
+HEADS_TILE = N_TILE // HEAD
+CHUNKS = E // N_TILE
+BN_MAX = 512
+QUANT = 1024
+
+FLOPS = 2 * IMAGES * TOKENS * E * 3 * E
+
+
+def tile_functatransformer_pa_kernel(
+    tc, x, ln1_g, ln1_b, Wq, bq, Wk, bk, Wv, bv, out_0, out_1, out_2
+):
+    nc = tc.nc
+    weights = [Wq, Wk, Wv]
+    biases = [bq, bk, bv]
+    outs = [out_0, out_1, out_2]
+    factors = [HEAD**-0.5, 1.0, 1.0]
+    all_bands = IMAGES * BANDS
+    all_chunks = 3 * CHUNKS
+
+    with tc.manual_schedule(), tc.tile_pool(name="keep", bufs=1) as keep, tc.tile_pool(
+        name="regroup", bufs=4
+    ) as regroup:
+        ident_bf = keep.tile([P, P], BF16)
+        make_identity(nc, ident_bf[:])
+        ident_f = keep.tile([P, P], F32)
+        make_identity(nc, ident_f[:])
+        to_window = keep.tile([P, P], F32)
+        by_image = ident_f[:].rearrange("p (r g l) -> p l g r", r=WIN, g=2, l=WIN)
+        by_window = to_window[:].rearrange("p (l g r) -> p l g r", l=WIN, g=2, r=WIN)
+        nc.vector.tensor_copy(out=by_window[:, 0:SHIFT, :, :], in_=by_image[:, SHIFT:WIN, :, :])
+        for g in range(2):
+            nc.vector.tensor_copy(out=by_window[:, SHIFT:WIN, g, :], in_=by_image[:, 0:SHIFT, 1 - g, :])
+        eps = keep.tile([P, 1], F32)
+        nc.vector.memset(eps[:], EPS)
+
+        x_codes = keep.tile([P, PASSES, IMAGES * TOKENS], U32, align_bytes=64)
+        x_scales = keep.tile([P, PASSES, IMAGES * TOKENS], U8, align_bytes=64)
+        w_codes = keep.tile([P, PASSES, 3 * E], U32, align_bytes=64)
+        w_scales = keep.tile([P, PASSES, 3 * E], U8, align_bytes=64)
+        bias_bf = keep.tile([P, 3, E], BF16)
+        bias_f = keep.tile([P, 3, E], F32)
+        gain_bf = keep.tile([P, PASSES, PACK], BF16)
+        shift_bf = keep.tile([P, PASSES, PACK], BF16)
+        gain = keep.tile([P, SLICES], F32)
+        shift = keep.tile([P, SLICES], F32)
+        w_raw = {}
+        grouped_w = {}
+
+        def regroup_weights(n, c):
+            m, half = divmod(n, CHUNKS)
+            grouped_w[(n, c)] = regroup.tile([P, N_TILE, PACK], BF16, name="grouped_w", align_bytes=64)
+            copy = nc.vector.tensor_copy if n == 0 else nc.scalar.copy
+            copy(
+                out=grouped_w[(n, c)][:].rearrange("p (u i) j -> p u j i", i=4),
+                in_=w_raw[(m, c)][:, :, N_TILE * half : N_TILE * (half + 1)].rearrange("p j (u i) -> p u j i", i=4),
+            )
+
+        def quantise_weights(n, c):
+            nc.vector.quantize_mx(
+                out=w_codes[:, c, N_TILE * n : N_TILE * (n + 1)].bitcast(FP8X4),
+                scales=w_scales[:, c, N_TILE * n : N_TILE * (n + 1)],
+                in_=grouped_w[(n, c)][:].rearrange("p n j -> p (n j)"),
+            )
+
+        with tc.tile_pool(name="norm", bufs=1) as norm, tc.tile_pool(
+            name="centred", bufs=all_bands
+        ) as centred, tc.tile_pool(name="small", bufs=all_bands) as small, tc.psum_pool(
+            name="tokens_first", bufs=3
+        ) as tokens_first, tc.psum_pool(name="channels_first", bufs=4) as channels_first:
+            x_sb = norm.tile([P, IMAGES, SLICES, TOKENS], BF16)
+            for b in range(IMAGES):
+                for c in range(PASSES):
+                    nc.sync.dma_start(
+                        out=x_sb[:, b, PACK * c : PACK * (c + 1), :],
+                        in_=x[b, K_PASS * c : K_PASS * (c + 1)].rearrange("(p j) r k -> p j (r k)", j=PACK),
+                    )
+            with nc.allow_non_contiguous_dma(reason="two small vectors, 4 channels to a partition"):
+                nc.sync.dma_start(out=gain_bf[:], in_=ln1_g.rearrange("(c p j) -> p c j", c=PASSES, j=PACK))
+                nc.sync.dma_start(out=shift_bf[:], in_=ln1_b.rearrange("(c p j) -> p c j", c=PASSES, j=PACK))
+            for m in range(3):
+                for c in range(PASSES):
+                    w_raw[(m, c)] = keep.tile([P, PACK, E], BF16, name="w_raw_%d_%d" % (m, c))
+                    nc.sync.dma_start(
+                        out=w_raw[(m, c)][:],
+                        in_=weights[m][K_PASS * c : K_PASS * (c + 1), :].rearrange("(p j) n -> p j n", j=PACK),
+                    )
+                nc.sync.dma_start(out=bias_bf[:, m, :], in_=biases[m].partition_broadcast(P))
+
+            first = SHIFT * COLS
+            x_last = norm.tile([P, IMAGES, SLICES, BLOCK], BF16)
+            for b in range(IMAGES):
+                nc.gpsimd.tensor_scalar(
+                    out=x_last[:, b, :, 0 : BLOCK - first], in0=x_sb[:, b, :, TOKENS - (BLOCK - first) : TOKENS],
+                    scalar1=1.0, scalar2=0.0, op0=ALU.mult, op1=ALU.add,
+                )
+                nc.gpsimd.tensor_scalar(
+                    out=x_last[:, b, :, BLOCK - first : BLOCK], in0=x_sb[:, b, :, 0:first],
+                    scalar1=1.0, scalar2=0.0, op0=ALU.mult, op1=ALU.add,
+                )
+            for m in range(3):
+                nc.gpsimd.tensor_scalar(
+                    out=bias_f[:, m, :], in0=bias_bf[:, m, :], scalar1=factors[m], scalar2=0.0,
+                    op0=ALU.mult, op1=ALU.add,
+                )
+
+            normed = norm.tile([P, SLICES, WIN, all_bands * RUN], BF16)
+            grouped_x = norm.tile([P, PASSES, WIN, all_bands * RUN, PACK], BF16, align_bytes=64)
+            xt_flat = {}
+            mean_var = {}
+            std = {}
+            z = {}
+
+            def tokens_first_and_statistics(t):
+                b, a = divmod(t, BANDS)
+                xt = tokens_first.tile([P, SLICES, P], BF16, name="xt")
+                for s in range(SLICES):
+                    if a < BANDS - 1:
+                        band = x_sb[:, b, s, BLOCK * a + first : BLOCK * (a + 1) + first]
+                    else:
+                        band = x_last[:, b, s, :]
+                    nc.tensor.transpose(xt[:, s, :], band, ident_bf[:])
+                xt_flat[t] = xt[:].rearrange("t s p -> t (s p)")
+                stats = small.tile([P, E // BN_MAX, 6], F32, name="stats")
+                for i in range(E // BN_MAX):
+                    nc.vector.bn_stats(out=stats[:, i, :], in_=xt_flat[t][:, BN_MAX * i : BN_MAX * (i + 1)])
+                mean_var[t] = small.tile([P, 2], F32, name="mean_var")
+                nc.vector.bn_aggr(out=mean_var[t][:], in_=stats[:].rearrange("t i v -> t (i v)"))
+                std[t] = small.tile([P, 1], F32, name="std")
+                nc.scalar.activation(out=std[t][:], in_=mean_var[t][:, 1:2], func=ACT.Sqrt, bias=eps[:, 0:1], scale=1.0)
+
+            def centre_and_scale(t):
+                rstd = small.tile([P, 1], F32, name="rstd")
+                nc.vector.reciprocal(out=rstd[:], in_=std[t][:])
+                offset = small.tile([P, 1], F32, name="offset")
+                nc.vector.scalar_tensor_tensor(
+                    out=offset[:], in0=mean_var[t][:, 0:1], scalar=-1.0, in1=rstd[:], op0=ALU.mult, op1=ALU.mult
+                )
+                z[t] = centred.tile([P, E], F32, name="z")
+                nc.scalar.activation(out=z[t][:], in_=xt_flat[t], func=ACT.Identity, bias=offset[:, 0:1], scale=rstd[:, 0:1])
+
+            def channels_first_gain_shift(b, s, on_scalar):
+                zt = channels_first.tile([P, BANDS, P], F32, name="zt")
+                for a in range(BANDS):
+                    nc.tensor.transpose(zt[:, a, :], z[BANDS * b + a][:, P * s : P * (s + 1)], to_window[:])
+                zt_by_l = zt[:].rearrange("p a (l t) -> p l a t", l=WIN)
+                normed_s = normed[:, s, :, BANDS * RUN * b : BANDS * RUN * (b + 1)].rearrange("p l (a t) -> p l a t", a=BANDS)
+                if on_scalar:
+                    nc.scalar.activation(
+                        out=normed_s, in_=zt_by_l, func=ACT.Identity, bias=shift[:, s : s + 1], scale=gain[:, s : s + 1]
+                    )
+                else:
+                    nc.vector.tensor_scalar(
+                        out=normed_s, in0=zt_by_l, scalar1=gain[:, s : s + 1], scalar2=shift[:, s : s + 1],
+                        op0=ALU.mult, op1=ALU.add,
+                    )
+
+            def group_words(b, c):
+                tokens_b = slice(BANDS * RUN * b, BANDS * RUN * (b + 1))
+                nc.vector.tensor_copy(
+                    out=grouped_x[:, c, :, tokens_b, :].rearrange("p l (u i) j -> p l u j i", i=4),
+                    in_=normed[:, PACK * c : PACK * (c + 1), :, tokens_b].rearrange("p j l (u i) -> p l u j i", i=4),
+                )
+
+            beside = SLICES // BANDS
+            for t in range(all_bands):
+                tokens_first_and_statistics(t)
+                if t >= 1:
+                    centre_and_scale(t - 1)
+                if t == BANDS:
+                    nc.vector.tensor_copy(out=gain[:], in_=gain_bf[:].rearrange("p c j -> p (c j)"))
+                    nc.vector.tensor_copy(out=shift[:], in_=shift_bf[:].rearrange("p c j -> p (c j)"))
+                if t >= BANDS:
+                    for s in range(beside * (t - BANDS), beside * (t - BANDS + 1)):
+                        channels_first_gain_shift(0, s, s % 2 == 0)
+            centre_and_scale(all_bands - 1)
+            for c in range(PASSES):
+                group_words(0, c)
+            for c in range(PASSES):
+                regroup_weights(0, c)
+            for c in range(PASSES):
+                quantise_weights(0, c)
+            for s in range(SLICES):
+                channels_first_gain_shift(1, s, True)
+                if s % PACK == PACK - 1:
+                    group_words(1, s // PACK)
+
+            per_call = QUANT // PACK
+            for i in range(IMAGES * TOKENS // per_call):
+                for c in range(PASSES):
+                    nc.vector.quantize_mx(
+                        out=x_codes[:, c, per_call * i : per_call * (i + 1)].bitcast(FP8X4),
+                        scales=x_scales[:, c, per_call * i : per_call * (i + 1)],
+                        in_=grouped_x[:, c, (per_call // P) * i : (per_call // P) * (i + 1), :, :].rearrange(
+                            "p l t j -> p (l t j)"
+                        ),
+                    )
+
+        with tc.tile_pool(name="stage", bufs=3, reuse_waits="tile") as stage, tc.psum_pool(
+            name="sums", bufs=8, reuse_waits="tile"
+        ) as sums:
+            for n in range(all_chunks):
+                m, half = divmod(n, CHUNKS)
+                if n + 1 < all_chunks:
+                    for c in range(PASSES):
+                        regroup_weights(n + 1, c)
+                staged = stage.tile([P, HEADS_TILE, WIN, HEAD], F32, name="staged")
+                for l in range(WIN):
+                    acc = sums.tile([P, N_TILE], F32, name="acc")
+                    for c in range(PASSES):
+                        nc.tensor.matmul_mx(
+                            out=acc[:],
+                            lhsT=x_codes[:, c, P * l : P * (l + 1)].bitcast(FP8X4),
+                            lhsT_scale=x_scales[:, c, P * l : P * (l + 1)],
+                            rhs=w_codes[:, c, N_TILE * n : N_TILE * (n + 1)].bitcast(FP8X4),
+                            rhs_scale=w_scales[:, c, N_TILE * n : N_TILE * (n + 1)],
+                            start=(c == 0),
+                            stop=(c == PASSES - 1),
+                        )
+                    nc.vector.scalar_tensor_tensor(
+                        out=staged[:, :, l, :],
+                        in0=acc[:].rearrange("p (h d) -> p h d", d=HEAD),
+                        scalar=factors[m],
+                        in1=bias_f[:, m, N_TILE * half : N_TILE * (half + 1)].rearrange("p (h d) -> p h d", d=HEAD),
+                        op0=ALU.mult,
+                        op1=ALU.add,
+                    )
+                    if l < PASSES and n + 1 < all_chunks:
+                        quantise_weights(n + 1, l)
+                by_head = outs[m].rearrange("b w h (r l) d -> h (b w) r (l d)", r=WIN)
+                for h in range(HEADS_TILE):
+                    nc.sync.dma_start(
+                        out=by_head[HEADS_TILE * half + h],
+                        in_=staged[:, h, :, :].rearrange("p l d -> p (l d)"),
+                    )

@@ -28,7 +28,12 @@ RUN = (COLS // WIN) * WIN
 N_TILE = 512
 HEADS_TILE = N_TILE // HEAD
 CHUNKS = E // N_TILE
+N_MX = 128
+HEADS_MX = N_MX // HEAD
+L_BANK = N_TILE // N_MX
+assert WIN // L_BANK == PASSES
 BN_MAX = 512
+AHEAD = 2
 QUANT = 1024
 
 FLOPS = 2 * IMAGES * TOKENS * E * 3 * E
@@ -41,7 +46,6 @@ def tile_functatransformer_pa_kernel(
     weights = [Wq, Wk, Wv]
     biases = [bq, bk, bv]
     outs = [out_0, out_1, out_2]
-    factors = [HEAD**-0.5, 1.0, 1.0]
     all_bands = IMAGES * BANDS
     all_chunks = 3 * CHUNKS
 
@@ -93,8 +97,8 @@ def tile_functatransformer_pa_kernel(
         with tc.tile_pool(name="norm", bufs=1) as norm, tc.tile_pool(
             name="centred", bufs=all_bands
         ) as centred, tc.tile_pool(name="small", bufs=all_bands) as small, tc.psum_pool(
-            name="tokens_first", bufs=3
-        ) as tokens_first, tc.psum_pool(name="channels_first", bufs=4) as channels_first:
+            name="tokens_first", bufs=4
+        ) as tokens_first_pool, tc.psum_pool(name="channels_first", bufs=4) as channels_first:
             x_sb = norm.tile([P, IMAGES, SLICES, TOKENS], BF16)
             for b in range(IMAGES):
                 for c in range(PASSES):
@@ -127,7 +131,7 @@ def tile_functatransformer_pa_kernel(
                 )
             for m in range(3):
                 nc.gpsimd.tensor_scalar(
-                    out=bias_f[:, m, :], in0=bias_bf[:, m, :], scalar1=factors[m], scalar2=0.0,
+                    out=bias_f[:, m, :], in0=bias_bf[:, m, :], scalar1=1.0, scalar2=0.0,
                     op0=ALU.mult, op1=ALU.add,
                 )
 
@@ -138,9 +142,9 @@ def tile_functatransformer_pa_kernel(
             std = {}
             z = {}
 
-            def tokens_first_and_statistics(t):
+            def tokens_first(t):
                 b, a = divmod(t, BANDS)
-                xt = tokens_first.tile([P, SLICES, P], BF16, name="xt")
+                xt = tokens_first_pool.tile([P, SLICES, P], BF16, name="xt")
                 for s in range(SLICES):
                     if a < BANDS - 1:
                         band = x_sb[:, b, s, BLOCK * a + first : BLOCK * (a + 1) + first]
@@ -148,6 +152,8 @@ def tile_functatransformer_pa_kernel(
                         band = x_last[:, b, s, :]
                     nc.tensor.transpose(xt[:, s, :], band, ident_bf[:])
                 xt_flat[t] = xt[:].rearrange("t s p -> t (s p)")
+
+            def statistics(t):
                 stats = small.tile([P, E // BN_MAX, 6], F32, name="stats")
                 for i in range(E // BN_MAX):
                     nc.vector.bn_stats(out=stats[:, i, :], in_=xt_flat[t][:, BN_MAX * i : BN_MAX * (i + 1)])
@@ -190,8 +196,12 @@ def tile_functatransformer_pa_kernel(
                 )
 
             beside = SLICES // BANDS
+            for t in range(AHEAD):
+                tokens_first(t)
             for t in range(all_bands):
-                tokens_first_and_statistics(t)
+                if t + AHEAD < all_bands:
+                    tokens_first(t + AHEAD)
+                statistics(t)
                 if t >= 1:
                     centre_and_scale(t - 1)
                 if t == BANDS:
@@ -223,40 +233,51 @@ def tile_functatransformer_pa_kernel(
                         ),
                     )
 
-        with tc.tile_pool(name="stage", bufs=3, reuse_waits="tile") as stage, tc.psum_pool(
+        with tc.tile_pool(name="stage", bufs=8, reuse_waits="tile") as stage, tc.psum_pool(
             name="sums", bufs=8, reuse_waits="tile"
         ) as sums:
             for n in range(all_chunks):
                 m, half = divmod(n, CHUNKS)
+                by_head = outs[m].rearrange("b w h (r l) d -> h (b w) r (l d)", r=WIN)
                 if n + 1 < all_chunks:
                     for c in range(PASSES):
                         regroup_weights(n + 1, c)
-                staged = stage.tile([P, HEADS_TILE, WIN, HEAD], F32, name="staged")
-                for l in range(WIN):
-                    acc = sums.tile([P, N_TILE], F32, name="acc")
-                    for c in range(PASSES):
-                        nc.tensor.matmul_mx(
-                            out=acc[:],
-                            lhsT=x_codes[:, c, P * l : P * (l + 1)].bitcast(FP8X4),
-                            lhsT_scale=x_scales[:, c, P * l : P * (l + 1)],
-                            rhs=w_codes[:, c, N_TILE * n : N_TILE * (n + 1)].bitcast(FP8X4),
-                            rhs_scale=w_scales[:, c, N_TILE * n : N_TILE * (n + 1)],
-                            start=(c == 0),
-                            stop=(c == PASSES - 1),
+                for q in range(N_TILE // N_MX):
+                    w_cols = slice(N_TILE * n + N_MX * q, N_TILE * n + N_MX * (q + 1))
+                    bias_cols = slice(N_TILE * half + N_MX * q, N_TILE * half + N_MX * (q + 1))
+                    staged = stage.tile([P, HEADS_MX, WIN, HEAD], F32, name="staged")
+                    for k in range(WIN // L_BANK):
+                        acc = sums.tile([P, L_BANK, N_MX], F32, name="acc")
+                        for i in range(L_BANK):
+                            tokens_l = slice(P * (L_BANK * k + i), P * (L_BANK * k + i + 1))
+                            for c in range(PASSES):
+                                nc.tensor.matmul_mx(
+                                    out=acc[:, i, :],
+                                    lhsT=x_codes[:, c, tokens_l].bitcast(FP8X4),
+                                    lhsT_scale=x_scales[:, c, tokens_l],
+                                    rhs=w_codes[:, c, w_cols].bitcast(FP8X4),
+                                    rhs_scale=w_scales[:, c, w_cols],
+                                    start=(c == 0),
+                                    stop=(c == PASSES - 1),
+                                )
+                        nc.vector.tensor_tensor(
+                            out=staged[:, :, L_BANK * k : L_BANK * (k + 1), :],
+                            in0=acc[:].rearrange("p i (h d) -> p h i d", d=HEAD),
+                            in1=bias_f[:, m, bias_cols]
+                            .rearrange("p (h d) -> p h d", d=HEAD)
+                            .unsqueeze(2)
+                            .to_broadcast([P, HEADS_MX, L_BANK, HEAD]),
+                            op=ALU.add,
                         )
-                    nc.vector.scalar_tensor_tensor(
-                        out=staged[:, :, l, :],
-                        in0=acc[:].rearrange("p (h d) -> p h d", d=HEAD),
-                        scalar=factors[m],
-                        in1=bias_f[:, m, N_TILE * half : N_TILE * (half + 1)].rearrange("p (h d) -> p h d", d=HEAD),
-                        op0=ALU.mult,
-                        op1=ALU.add,
-                    )
-                    if l < PASSES and n + 1 < all_chunks:
-                        quantise_weights(n + 1, l)
-                by_head = outs[m].rearrange("b w h (r l) d -> h (b w) r (l d)", r=WIN)
-                for h in range(HEADS_TILE):
-                    nc.sync.dma_start(
-                        out=by_head[HEADS_TILE * half + h],
-                        in_=staged[:, h, :, :].rearrange("p l d -> p (l d)"),
-                    )
+                        if q == 0 and n + 1 < all_chunks:
+                            quantise_weights(n + 1, k)
+                    if m == 0:
+                        flat = staged[:].rearrange("p h l d -> p (h l d)")
+                        nc.gpsimd.tensor_scalar(
+                            out=flat, in0=flat, scalar1=HEAD**-0.5, scalar2=0.0, op0=ALU.mult, op1=ALU.add
+                        )
+                    for h in range(HEADS_MX):
+                        nc.sync.dma_start(
+                            out=by_head[HEADS_TILE * half + HEADS_MX * q + h],
+                            in_=staged[:, h, :, :].rearrange("p l d -> p (l d)"),
+                        )

@@ -33,6 +33,7 @@ HEADS_MX = N_MX // HEAD
 L_BANK = N_TILE // N_MX
 assert WIN // L_BANK == PASSES
 BN_MAX = 512
+RELIEF = 4
 AHEAD = 2
 QUANT = 1024
 
@@ -50,7 +51,7 @@ def tile_functatransformer_pa_kernel(
     all_chunks = 3 * CHUNKS
 
     with tc.manual_schedule(), tc.tile_pool(name="keep", bufs=1) as keep, tc.tile_pool(
-        name="regroup", bufs=4
+        name="regroup", bufs=6
     ) as regroup:
         ident_bf = keep.tile([P, P], BF16)
         make_identity(nc, ident_bf[:])
@@ -222,6 +223,9 @@ def tile_functatransformer_pa_kernel(
                 if s % PACK == PACK - 1:
                     group_words(1, s // PACK)
 
+            for c in range(PASSES):
+                regroup_weights(1, c)
+
             per_call = QUANT // PACK
             for i in range(IMAGES * TOKENS // per_call):
                 for c in range(PASSES):
@@ -233,16 +237,17 @@ def tile_functatransformer_pa_kernel(
                         ),
                     )
 
-        with tc.tile_pool(name="stage", bufs=8, reuse_waits="tile") as stage, tc.psum_pool(
+        with tc.tile_pool(name="stage", bufs=8, reuse_waits="tile") as stage, tc.tile_pool(
+            name="spare", bufs=3, reuse_waits="tile"
+        ) as spare, tc.psum_pool(
             name="sums", bufs=8, reuse_waits="tile"
         ) as sums:
             for n in range(all_chunks):
                 m, half = divmod(n, CHUNKS)
                 by_head = outs[m].rearrange("b w h (r l) d -> h (b w) r (l d)", r=WIN)
-                if n + 1 < all_chunks:
-                    for c in range(PASSES):
-                        regroup_weights(n + 1, c)
                 for q in range(N_TILE // N_MX):
+                    if q % 2 == 0 and n + 2 < all_chunks:
+                        regroup_weights(n + 2, q // 2)
                     w_cols = slice(N_TILE * n + N_MX * q, N_TILE * n + N_MX * (q + 1))
                     bias_cols = slice(N_TILE * half + N_MX * q, N_TILE * half + N_MX * (q + 1))
                     staged = stage.tile([P, HEADS_MX, WIN, HEAD], F32, name="staged")
@@ -260,15 +265,23 @@ def tile_functatransformer_pa_kernel(
                                     start=(c == 0),
                                     stop=(c == PASSES - 1),
                                 )
-                        nc.vector.tensor_tensor(
-                            out=staged[:, :, L_BANK * k : L_BANK * (k + 1), :],
-                            in0=acc[:].rearrange("p i (h d) -> p h i d", d=HEAD),
-                            in1=bias_f[:, m, bias_cols]
+                        staged_k = staged[:, :, L_BANK * k : L_BANK * (k + 1), :]
+                        bias_k = (
+                            bias_f[:, m, bias_cols]
                             .rearrange("p (h d) -> p h d", d=HEAD)
                             .unsqueeze(2)
-                            .to_broadcast([P, HEADS_MX, L_BANK, HEAD]),
-                            op=ALU.add,
+                            .to_broadcast([P, HEADS_MX, L_BANK, HEAD])
                         )
+                        if ((WIN // L_BANK) * q + k) % RELIEF == RELIEF - 1:
+                            plain = spare.tile([P, L_BANK, N_MX], F32, name="plain")
+                            nc.scalar.copy(out=plain[:], in_=acc[:])
+                            nc.gpsimd.tensor_tensor(
+                                out=staged_k, in0=plain[:].rearrange("p i (h d) -> p h i d", d=HEAD), in1=bias_k, op=ALU.add
+                            )
+                        else:
+                            nc.vector.tensor_tensor(
+                                out=staged_k, in0=acc[:].rearrange("p i (h d) -> p h i d", d=HEAD), in1=bias_k, op=ALU.add
+                            )
                         if q == 0 and n + 1 < all_chunks:
                             quantise_weights(n + 1, k)
                     if m == 0:

@@ -33,7 +33,6 @@ HEADS_MX = N_MX // HEAD
 L_BANK = N_TILE // N_MX
 assert WIN // L_BANK == PASSES
 BN_MAX = 512
-RELIEF = 4
 AHEAD = 2
 QUANT = 1024
 
@@ -51,7 +50,7 @@ def tile_functatransformer_pa_kernel(
     all_chunks = 3 * CHUNKS
 
     with tc.manual_schedule(), tc.tile_pool(name="keep", bufs=1) as keep, tc.tile_pool(
-        name="regroup", bufs=6
+        name="regroup", bufs=4
     ) as regroup:
         ident_bf = keep.tile([P, P], BF16)
         make_identity(nc, ident_bf[:])
@@ -196,35 +195,26 @@ def tile_functatransformer_pa_kernel(
                     in_=normed[:, PACK * c : PACK * (c + 1), :, tokens_b].rearrange("p j l (u i) -> p l u j i", i=4),
                 )
 
-            beside = SLICES // BANDS
             for t in range(AHEAD):
                 tokens_first(t)
-            for t in range(all_bands):
+            for t in range(all_bands + 1):
                 if t + AHEAD < all_bands:
                     tokens_first(t + AHEAD)
-                statistics(t)
+                if t < all_bands:
+                    statistics(t)
                 if t >= 1:
                     centre_and_scale(t - 1)
-                if t == BANDS:
-                    nc.vector.tensor_copy(out=gain[:], in_=gain_bf[:].rearrange("p c j -> p (c j)"))
-                    nc.vector.tensor_copy(out=shift[:], in_=shift_bf[:].rearrange("p c j -> p (c j)"))
-                if t >= BANDS:
-                    for s in range(beside * (t - BANDS), beside * (t - BANDS + 1)):
-                        channels_first_gain_shift(0, s, s % 2 == 0)
-            centre_and_scale(all_bands - 1)
-            for c in range(PASSES):
-                group_words(0, c)
+            nc.vector.tensor_copy(out=gain[:], in_=gain_bf[:].rearrange("p c j -> p (c j)"))
+            nc.vector.tensor_copy(out=shift[:], in_=shift_bf[:].rearrange("p c j -> p (c j)"))
             for c in range(PASSES):
                 regroup_weights(0, c)
             for c in range(PASSES):
                 quantise_weights(0, c)
-            for s in range(SLICES):
-                channels_first_gain_shift(1, s, True)
-                if s % PACK == PACK - 1:
-                    group_words(1, s // PACK)
-
-            for c in range(PASSES):
-                regroup_weights(1, c)
+            for b in range(IMAGES):
+                for s in range(SLICES):
+                    channels_first_gain_shift(b, s, s % PACK != PACK - 1)
+                    if s % PACK == PACK - 1:
+                        group_words(b, s // PACK)
 
             per_call = QUANT // PACK
             for i in range(IMAGES * TOKENS // per_call):
@@ -237,17 +227,16 @@ def tile_functatransformer_pa_kernel(
                         ),
                     )
 
-        with tc.tile_pool(name="stage", bufs=8, reuse_waits="tile") as stage, tc.tile_pool(
-            name="spare", bufs=3, reuse_waits="tile"
-        ) as spare, tc.psum_pool(
+        with tc.tile_pool(name="stage", bufs=8, reuse_waits="tile") as stage, tc.psum_pool(
             name="sums", bufs=8, reuse_waits="tile"
         ) as sums:
             for n in range(all_chunks):
                 m, half = divmod(n, CHUNKS)
                 by_head = outs[m].rearrange("b w h (r l) d -> h (b w) r (l d)", r=WIN)
+                if n + 1 < all_chunks:
+                    for c in range(PASSES):
+                        regroup_weights(n + 1, c)
                 for q in range(N_TILE // N_MX):
-                    if q % 2 == 0 and n + 2 < all_chunks:
-                        regroup_weights(n + 2, q // 2)
                     w_cols = slice(N_TILE * n + N_MX * q, N_TILE * n + N_MX * (q + 1))
                     bias_cols = slice(N_TILE * half + N_MX * q, N_TILE * half + N_MX * (q + 1))
                     staged = stage.tile([P, HEADS_MX, WIN, HEAD], F32, name="staged")
@@ -265,23 +254,15 @@ def tile_functatransformer_pa_kernel(
                                     start=(c == 0),
                                     stop=(c == PASSES - 1),
                                 )
-                        staged_k = staged[:, :, L_BANK * k : L_BANK * (k + 1), :]
-                        bias_k = (
-                            bias_f[:, m, bias_cols]
+                        nc.vector.tensor_tensor(
+                            out=staged[:, :, L_BANK * k : L_BANK * (k + 1), :],
+                            in0=acc[:].rearrange("p i (h d) -> p h i d", d=HEAD),
+                            in1=bias_f[:, m, bias_cols]
                             .rearrange("p (h d) -> p h d", d=HEAD)
                             .unsqueeze(2)
-                            .to_broadcast([P, HEADS_MX, L_BANK, HEAD])
+                            .to_broadcast([P, HEADS_MX, L_BANK, HEAD]),
+                            op=ALU.add,
                         )
-                        if ((WIN // L_BANK) * q + k) % RELIEF == RELIEF - 1:
-                            plain = spare.tile([P, L_BANK, N_MX], F32, name="plain")
-                            nc.scalar.copy(out=plain[:], in_=acc[:])
-                            nc.gpsimd.tensor_tensor(
-                                out=staged_k, in0=plain[:].rearrange("p i (h d) -> p h i d", d=HEAD), in1=bias_k, op=ALU.add
-                            )
-                        else:
-                            nc.vector.tensor_tensor(
-                                out=staged_k, in0=acc[:].rearrange("p i (h d) -> p h i d", d=HEAD), in1=bias_k, op=ALU.add
-                            )
                         if q == 0 and n + 1 < all_chunks:
                             quantise_weights(n + 1, k)
                     if m == 0:

@@ -47,7 +47,8 @@ def tile_functatransformer_pa_kernel(
     biases = [bq, bk, bv]
     outs = [out_0, out_1, out_2]
     all_bands = IMAGES * BANDS
-    all_chunks = 3 * CHUNKS
+    chunk_of = [(1, 0), (1, 1), (2, 0), (0, 0), (0, 1), (2, 1)]
+    all_chunks = len(chunk_of)
 
     with tc.manual_schedule(), tc.tile_pool(name="keep", bufs=1) as keep, tc.tile_pool(
         name="regroup", bufs=4
@@ -70,7 +71,6 @@ def tile_functatransformer_pa_kernel(
         w_codes = keep.tile([P, PASSES, 3 * E], U32, align_bytes=64)
         w_scales = keep.tile([P, PASSES, 3 * E], U8, align_bytes=64)
         bias_bf = keep.tile([P, 3, E], BF16)
-        bias_f = keep.tile([P, 3, E], F32)
         gain_bf = keep.tile([P, PASSES, PACK], BF16)
         shift_bf = keep.tile([P, PASSES, PACK], BF16)
         gain = keep.tile([P, SLICES], F32)
@@ -79,7 +79,7 @@ def tile_functatransformer_pa_kernel(
         grouped_w = {}
 
         def regroup_weights(n, c):
-            m, half = divmod(n, CHUNKS)
+            m, half = chunk_of[n]
             grouped_w[(n, c)] = regroup.tile([P, N_TILE, PACK], BF16, name="grouped_w", align_bytes=64)
             copy = nc.vector.tensor_copy if n == 0 else nc.scalar.copy
             copy(
@@ -109,7 +109,7 @@ def tile_functatransformer_pa_kernel(
             with nc.allow_non_contiguous_dma(reason="two small vectors, 4 channels to a partition"):
                 nc.sync.dma_start(out=gain_bf[:], in_=ln1_g.rearrange("(c p j) -> p c j", c=PASSES, j=PACK))
                 nc.sync.dma_start(out=shift_bf[:], in_=ln1_b.rearrange("(c p j) -> p c j", c=PASSES, j=PACK))
-            for m in range(3):
+            for m in (1, 2, 0):
                 for c in range(PASSES):
                     w_raw[(m, c)] = keep.tile([P, PACK, E], BF16, name="w_raw_%d_%d" % (m, c))
                     nc.sync.dma_start(
@@ -128,11 +128,6 @@ def tile_functatransformer_pa_kernel(
                 nc.gpsimd.tensor_scalar(
                     out=x_last[:, b, :, BLOCK - first : BLOCK], in0=x_sb[:, b, :, 0:first],
                     scalar1=1.0, scalar2=0.0, op0=ALU.mult, op1=ALU.add,
-                )
-            for m in range(3):
-                nc.gpsimd.tensor_scalar(
-                    out=bias_f[:, m, :], in0=bias_bf[:, m, :], scalar1=1.0, scalar2=0.0,
-                    op0=ALU.mult, op1=ALU.add,
                 )
 
             normed = norm.tile([P, SLICES, WIN, all_bands * RUN], BF16)
@@ -230,12 +225,14 @@ def tile_functatransformer_pa_kernel(
         with tc.tile_pool(name="stage", bufs=8, reuse_waits="tile") as stage, tc.psum_pool(
             name="sums", bufs=8, reuse_waits="tile"
         ) as sums:
+            for c in range(PASSES):
+                regroup_weights(1, c)
             for n in range(all_chunks):
-                m, half = divmod(n, CHUNKS)
+                m, half = chunk_of[n]
                 by_head = outs[m].rearrange("b w h (r l) d -> h (b w) r (l d)", r=WIN)
-                if n + 1 < all_chunks:
+                if n + 2 < all_chunks:
                     for c in range(PASSES):
-                        regroup_weights(n + 1, c)
+                        regroup_weights(n + 2, c)
                 for q in range(N_TILE // N_MX):
                     w_cols = slice(N_TILE * n + N_MX * q, N_TILE * n + N_MX * (q + 1))
                     bias_cols = slice(N_TILE * half + N_MX * q, N_TILE * half + N_MX * (q + 1))
@@ -257,7 +254,7 @@ def tile_functatransformer_pa_kernel(
                         nc.vector.tensor_tensor(
                             out=staged[:, :, L_BANK * k : L_BANK * (k + 1), :],
                             in0=acc[:].rearrange("p i (h d) -> p h i d", d=HEAD),
-                            in1=bias_f[:, m, bias_cols]
+                            in1=bias_bf[:, m, bias_cols]
                             .rearrange("p (h d) -> p h d", d=HEAD)
                             .unsqueeze(2)
                             .to_broadcast([P, HEADS_MX, L_BANK, HEAD]),
@@ -267,9 +264,7 @@ def tile_functatransformer_pa_kernel(
                             quantise_weights(n + 1, k)
                     if m == 0:
                         flat = staged[:].rearrange("p h l d -> p (h l d)")
-                        nc.gpsimd.tensor_scalar(
-                            out=flat, in0=flat, scalar1=HEAD**-0.5, scalar2=0.0, op0=ALU.mult, op1=ALU.add
-                        )
+                        nc.scalar.activation(out=flat, in_=flat, func=ACT.Copy, scale=HEAD**-0.5)
                     for h in range(HEADS_MX):
                         nc.sync.dma_start(
                             out=by_head[HEADS_TILE * half + HEADS_MX * q + h],

@@ -148,24 +148,34 @@ def tile_functatransformer_pa_kernel(
                     nc.tensor.transpose(xt[:, s, :], band, ident_bf[:])
                 xt_flat[t] = xt[:].rearrange("t s p -> t (s p)")
 
-            def statistics(t):
-                stats = small.tile([P, E // BN_MAX, 6], F32, name="stats")
-                for i in range(E // BN_MAX):
-                    nc.vector.bn_stats(out=stats[:, i, :], in_=xt_flat[t][:, BN_MAX * i : BN_MAX * (i + 1)])
+            stats = {}
+            rstd = {}
+            assert E // BN_MAX == 2
+
+            def half_statistics(t, i):
+                if i == 0:
+                    stats[t] = small.tile([P, E // BN_MAX, 6], F32, name="stats")
+                nc.vector.bn_stats(out=stats[t][:, i, :], in_=xt_flat[t][:, BN_MAX * i : BN_MAX * (i + 1)])
+
+            def deviation(t):
                 mean_var[t] = small.tile([P, 2], F32, name="mean_var")
-                nc.vector.bn_aggr(out=mean_var[t][:], in_=stats[:].rearrange("t i v -> t (i v)"))
+                nc.vector.bn_aggr(out=mean_var[t][:], in_=stats[t][:].rearrange("t i v -> t (i v)"))
                 std[t] = small.tile([P, 1], F32, name="std")
                 nc.scalar.activation(out=std[t][:], in_=mean_var[t][:, 1:2], func=ACT.Sqrt, bias=eps[:, 0:1], scale=1.0)
 
+            def inverse(t):
+                rstd[t] = small.tile([P, 1], F32, name="rstd")
+                nc.vector.reciprocal(out=rstd[t][:], in_=std[t][:])
+
             def centre_and_scale(t):
-                rstd = small.tile([P, 1], F32, name="rstd")
-                nc.vector.reciprocal(out=rstd[:], in_=std[t][:])
                 offset = small.tile([P, 1], F32, name="offset")
                 nc.vector.scalar_tensor_tensor(
-                    out=offset[:], in0=mean_var[t][:, 0:1], scalar=-1.0, in1=rstd[:], op0=ALU.mult, op1=ALU.mult
+                    out=offset[:], in0=mean_var[t][:, 0:1], scalar=-1.0, in1=rstd[t][:], op0=ALU.mult, op1=ALU.mult
                 )
                 z[t] = centred.tile([P, E], F32, name="z")
-                nc.scalar.activation(out=z[t][:], in_=xt_flat[t], func=ACT.Identity, bias=offset[:, 0:1], scale=rstd[:, 0:1])
+                nc.scalar.activation(
+                    out=z[t][:], in_=xt_flat[t], func=ACT.Identity, bias=offset[:, 0:1], scale=rstd[t][:, 0:1]
+                )
 
             def channels_first_gain_shift(b, s, on_scalar):
                 zt = channels_first.tile([P, BANDS, P], F32, name="zt")
@@ -192,22 +202,30 @@ def tile_functatransformer_pa_kernel(
 
             for t in range(AHEAD):
                 tokens_first(t)
-            for t in range(all_bands + 1):
+            for t in range(all_bands + 2):
                 if t + AHEAD < all_bands:
                     tokens_first(t + AHEAD)
                 if t < all_bands:
-                    statistics(t)
-                if t >= 1:
-                    centre_and_scale(t - 1)
-            nc.vector.tensor_copy(out=gain[:], in_=gain_bf[:].rearrange("p c j -> p (c j)"))
-            nc.vector.tensor_copy(out=shift[:], in_=shift_bf[:].rearrange("p c j -> p (c j)"))
+                    half_statistics(t, 0)
+                if 1 <= t <= all_bands:
+                    deviation(t - 1)
+                if t == all_bands + 1:
+                    nc.vector.tensor_copy(out=shift[:], in_=shift_bf[:].rearrange("p c j -> p (c j)"))
+                if t >= 2:
+                    centre_and_scale(t - 2)
+                if t < all_bands:
+                    half_statistics(t, 1)
+                if t == all_bands:
+                    nc.vector.tensor_copy(out=gain[:], in_=gain_bf[:].rearrange("p c j -> p (c j)"))
+                if 1 <= t <= all_bands:
+                    inverse(t - 1)
             for c in range(PASSES):
                 regroup_weights(0, c)
             for c in range(PASSES):
                 quantise_weights(0, c)
             for b in range(IMAGES):
                 for s in range(SLICES):
-                    channels_first_gain_shift(b, s, s % PACK != PACK - 1)
+                    channels_first_gain_shift(b, s, s % PACK != PACK - 2)
                     if s % PACK == PACK - 1:
                         group_words(b, s // PACK)
 

@@ -100,12 +100,17 @@ def tile_functatransformer_pa_kernel(
             name="tokens_first", bufs=4
         ) as tokens_first_pool, tc.psum_pool(name="channels_first", bufs=4) as channels_first:
             x_sb = norm.tile([P, IMAGES, SLICES, TOKENS], BF16)
+            first = SHIFT * COLS
             for b in range(IMAGES):
-                for c in range(PASSES):
-                    nc.sync.dma_start(
-                        out=x_sb[:, b, PACK * c : PACK * (c + 1), :],
-                        in_=x[b, K_PASS * c : K_PASS * (c + 1)].rearrange("(p j) r k -> p j (r k)", j=PACK),
-                    )
+                for lo, hi in ((0, 2 * BLOCK), (2 * BLOCK, TOKENS - first), (TOKENS - first, TOKENS)):
+                    source = (lo + first) % TOKENS
+                    for c in range(PASSES):
+                        nc.sync.dma_start(
+                            out=x_sb[:, b, PACK * c : PACK * (c + 1), lo:hi],
+                            in_=x[b, K_PASS * c : K_PASS * (c + 1)].rearrange("(p j) r k -> p j (r k)", j=PACK)[
+                                :, :, source : source + hi - lo
+                            ],
+                        )
             with nc.allow_non_contiguous_dma(reason="two small vectors, 4 channels to a partition"):
                 nc.sync.dma_start(out=gain_bf[:], in_=ln1_g.rearrange("(c p j) -> p c j", c=PASSES, j=PACK))
                 nc.sync.dma_start(out=shift_bf[:], in_=ln1_b.rearrange("(c p j) -> p c j", c=PASSES, j=PACK))
@@ -118,18 +123,6 @@ def tile_functatransformer_pa_kernel(
                     )
                 nc.sync.dma_start(out=bias_bf[:, m, :], in_=biases[m].partition_broadcast(P))
 
-            first = SHIFT * COLS
-            x_last = norm.tile([P, IMAGES, SLICES, BLOCK], BF16)
-            for b in range(IMAGES):
-                nc.gpsimd.tensor_scalar(
-                    out=x_last[:, b, :, 0 : BLOCK - first], in0=x_sb[:, b, :, TOKENS - (BLOCK - first) : TOKENS],
-                    scalar1=1.0, scalar2=0.0, op0=ALU.mult, op1=ALU.add,
-                )
-                nc.gpsimd.tensor_scalar(
-                    out=x_last[:, b, :, BLOCK - first : BLOCK], in0=x_sb[:, b, :, 0:first],
-                    scalar1=1.0, scalar2=0.0, op0=ALU.mult, op1=ALU.add,
-                )
-
             normed = norm.tile([P, SLICES, WIN, all_bands * RUN], BF16)
             grouped_x = norm.tile([P, PASSES, WIN, all_bands * RUN, PACK], BF16, align_bytes=64)
             xt_flat = {}
@@ -141,11 +134,7 @@ def tile_functatransformer_pa_kernel(
                 b, a = divmod(t, BANDS)
                 xt = tokens_first_pool.tile([P, SLICES, P], BF16, name="xt")
                 for s in range(SLICES):
-                    if a < BANDS - 1:
-                        band = x_sb[:, b, s, BLOCK * a + first : BLOCK * (a + 1) + first]
-                    else:
-                        band = x_last[:, b, s, :]
-                    nc.tensor.transpose(xt[:, s, :], band, ident_bf[:])
+                    nc.tensor.transpose(xt[:, s, :], x_sb[:, b, s, BLOCK * a : BLOCK * (a + 1)], ident_bf[:])
                 xt_flat[t] = xt[:].rearrange("t s p -> t (s p)")
 
             stats = {}

@@ -29,6 +29,8 @@ N_TILE = 512
 HEADS_TILE = N_TILE // HEAD
 CHUNKS = E // N_TILE
 N_MX = 128
+N_MX_Q = 256
+FACTOR = HEAD**-0.5
 HEADS_MX = N_MX // HEAD
 L_BANK = N_TILE // N_MX
 assert WIN // L_BANK == PASSES
@@ -71,6 +73,7 @@ def tile_functatransformer_pa_kernel(
         w_codes = keep.tile([P, PASSES, 3 * E], U32, align_bytes=64)
         w_scales = keep.tile([P, PASSES, 3 * E], U8, align_bytes=64)
         bias_bf = keep.tile([P, 3, E], BF16)
+        bias_q = keep.tile([P, E], F32)
         gain_bf = keep.tile([P, PASSES, PACK], BF16)
         shift_bf = keep.tile([P, PASSES, PACK], BF16)
         gain = keep.tile([P, SLICES], F32)
@@ -229,9 +232,9 @@ def tile_functatransformer_pa_kernel(
                         ),
                     )
 
-        with tc.tile_pool(name="stage", bufs=8, reuse_waits="tile") as stage, tc.psum_pool(
-            name="sums", bufs=8, reuse_waits="tile"
-        ) as sums:
+        with tc.tile_pool(name="stage", bufs=8, reuse_waits="tile") as stage, tc.tile_pool(
+            name="stage_q", bufs=3, reuse_waits="tile"
+        ) as stage_q, tc.psum_pool(name="sums", bufs=8, reuse_waits="tile") as sums:
             for c in range(PASSES):
                 regroup_weights(1, c)
             for n in range(all_chunks):
@@ -240,14 +243,22 @@ def tile_functatransformer_pa_kernel(
                 if n + 2 < all_chunks:
                     for c in range(PASSES):
                         regroup_weights(n + 2, c)
-                for q in range(N_TILE // N_MX):
-                    w_cols = slice(N_TILE * n + N_MX * q, N_TILE * n + N_MX * (q + 1))
-                    bias_cols = slice(N_TILE * half + N_MX * q, N_TILE * half + N_MX * (q + 1))
-                    staged = stage.tile([P, HEADS_MX, WIN, HEAD], F32, name="staged")
-                    for k in range(WIN // L_BANK):
-                        acc = sums.tile([P, L_BANK, N_MX], F32, name="acc")
-                        for i in range(L_BANK):
-                            tokens_l = slice(P * (L_BANK * k + i), P * (L_BANK * k + i + 1))
+                    if chunk_of[n + 2] == (0, 0):
+                        nc.scalar.activation(out=bias_q[:], in_=bias_bf[:, 0, :], func=ACT.Copy, scale=FACTOR)
+                n_mx = N_MX_Q if m == 0 else N_MX
+                heads_mx = n_mx // HEAD
+                l_bank = N_TILE // n_mx
+                for q in range(N_TILE // n_mx):
+                    w_cols = slice(N_TILE * n + n_mx * q, N_TILE * n + n_mx * (q + 1))
+                    bias_cols = slice(N_TILE * half + n_mx * q, N_TILE * half + n_mx * (q + 1))
+                    if m == 0:
+                        staged = stage_q.tile([P, heads_mx, WIN, HEAD], F32, name="staged_q")
+                    else:
+                        staged = stage.tile([P, heads_mx, WIN, HEAD], F32, name="staged")
+                    for k in range(WIN // l_bank):
+                        acc = sums.tile([P, l_bank, n_mx], F32, name="acc")
+                        for i in range(l_bank):
+                            tokens_l = slice(P * (l_bank * k + i), P * (l_bank * k + i + 1))
                             for c in range(PASSES):
                                 nc.tensor.matmul_mx(
                                     out=acc[:, i, :],
@@ -258,22 +269,30 @@ def tile_functatransformer_pa_kernel(
                                     start=(c == 0),
                                     stop=(c == PASSES - 1),
                                 )
-                        nc.vector.tensor_tensor(
-                            out=staged[:, :, L_BANK * k : L_BANK * (k + 1), :],
-                            in0=acc[:].rearrange("p i (h d) -> p h i d", d=HEAD),
-                            in1=bias_bf[:, m, bias_cols]
-                            .rearrange("p (h d) -> p h d", d=HEAD)
-                            .unsqueeze(2)
-                            .to_broadcast([P, HEADS_MX, L_BANK, HEAD]),
-                            op=ALU.add,
-                        )
-                        if q == 0 and n + 1 < all_chunks:
+                        if m == 0:
+                            for i in range(l_bank):
+                                nc.vector.scalar_tensor_tensor(
+                                    out=staged[:, :, l_bank * k + i, :],
+                                    in0=acc[:, i, :].rearrange("p (h d) -> p h d", d=HEAD),
+                                    scalar=FACTOR,
+                                    in1=bias_q[:, bias_cols].rearrange("p (h d) -> p h d", d=HEAD),
+                                    op0=ALU.mult,
+                                    op1=ALU.add,
+                                )
+                        else:
+                            nc.vector.tensor_tensor(
+                                out=staged[:, :, l_bank * k : l_bank * (k + 1), :],
+                                in0=acc[:].rearrange("p i (h d) -> p h i d", d=HEAD),
+                                in1=bias_bf[:, m, bias_cols]
+                                .rearrange("p (h d) -> p h d", d=HEAD)
+                                .unsqueeze(2)
+                                .to_broadcast([P, heads_mx, l_bank, HEAD]),
+                                op=ALU.add,
+                            )
+                        if q == 0 and k < PASSES and n + 1 < all_chunks:
                             quantise_weights(n + 1, k)
-                    if m == 0:
-                        flat = staged[:].rearrange("p h l d -> p (h l d)")
-                        nc.scalar.activation(out=flat, in_=flat, func=ACT.Copy, scale=HEAD**-0.5)
-                    for h in range(HEADS_MX):
+                    for h in range(heads_mx):
                         nc.sync.dma_start(
-                            out=by_head[HEADS_TILE * half + HEADS_MX * q + h],
+                            out=by_head[HEADS_TILE * half + heads_mx * q + h],
                             in_=staged[:, h, :, :].rearrange("p l d -> p (l d)"),
                         )

@@ -34,7 +34,8 @@ FACTOR = HEAD**-0.5
 HEADS_MX = N_MX // HEAD
 L_BANK = N_TILE // N_MX
 assert WIN // L_BANK == PASSES
-BN_MAX = 512
+PAD = 16
+ONES = 2
 AHEAD = 2
 QUANT = 1024
 
@@ -99,21 +100,24 @@ def tile_functatransformer_pa_kernel(
 
         with tc.tile_pool(name="norm", bufs=1) as norm, tc.tile_pool(
             name="centred", bufs=all_bands
-        ) as centred, tc.tile_pool(name="small", bufs=all_bands) as small, tc.psum_pool(
-            name="tokens_first", bufs=4
-        ) as tokens_first_pool, tc.psum_pool(name="channels_first", bufs=4) as channels_first:
-            x_sb = norm.tile([P, IMAGES, SLICES, TOKENS], BF16)
+        ) as centred, tc.tile_pool(name="small", bufs=all_bands) as small, tc.tile_pool(
+            name="scratch", bufs=2
+        ) as scratch, tc.psum_pool(name="moments", bufs=2) as moments_pool, tc.psum_pool(
+            name="tokens_first", bufs=3
+        ) as tokens_first_pool, tc.psum_pool(name="channels_first", bufs=3) as channels_first:
+            x_sb = norm.tile([P, IMAGES, SLICES, BANDS, BLOCK + PAD], BF16)
+            nc.vector.memset(x_sb[:, :, :, :, BLOCK : BLOCK + PAD].rearrange("p b s a k -> p (b s a) k"), 1.0)
             first = SHIFT * COLS
             for b in range(IMAGES):
-                for lo, hi in ((0, 2 * BLOCK), (2 * BLOCK, TOKENS - first), (TOKENS - first, TOKENS)):
-                    source = (lo + first) % TOKENS
+                for a in range(BANDS):
+                    start = BLOCK * a + first
+                    whole = min(BLOCK, TOKENS - start)
                     for c in range(PASSES):
-                        nc.sync.dma_start(
-                            out=x_sb[:, b, PACK * c : PACK * (c + 1), lo:hi],
-                            in_=x[b, K_PASS * c : K_PASS * (c + 1)].rearrange("(p j) r k -> p j (r k)", j=PACK)[
-                                :, :, source : source + hi - lo
-                            ],
-                        )
+                        source = x[b, K_PASS * c : K_PASS * (c + 1)].rearrange("(p j) r k -> p j (r k)", j=PACK)
+                        slices_c = slice(PACK * c, PACK * (c + 1))
+                        nc.sync.dma_start(out=x_sb[:, b, slices_c, a, 0:whole], in_=source[:, :, start : start + whole])
+                        if whole < BLOCK:
+                            nc.sync.dma_start(out=x_sb[:, b, slices_c, a, whole:BLOCK], in_=source[:, :, 0 : BLOCK - whole])
             with nc.allow_non_contiguous_dma(reason="two small vectors, 4 channels to a partition"):
                 nc.sync.dma_start(out=gain_bf[:], in_=ln1_g.rearrange("(c p j) -> p c j", c=PASSES, j=PACK))
                 nc.sync.dma_start(out=shift_bf[:], in_=ln1_b.rearrange("(c p j) -> p c j", c=PASSES, j=PACK))
@@ -128,46 +132,67 @@ def tile_functatransformer_pa_kernel(
 
             normed = norm.tile([P, SLICES, WIN, all_bands * RUN], BF16)
             grouped_x = norm.tile([P, PASSES, WIN, all_bands * RUN, PACK], BF16, align_bytes=64)
+            sums_of = {}
             xt_flat = {}
-            mean_var = {}
+            neg_mean = {}
             std = {}
             z = {}
+
+            def products_of_tokens(t):
+                b, a = divmod(t, BANDS)
+                sums_of[t] = moments_pool.tile([P, BLOCK + ONES], F32, name="sums_of")
+                for s in range(SLICES):
+                    nc.tensor.matmul(
+                        out=sums_of[t][:],
+                        lhsT=x_sb[:, b, s, a, 0:BLOCK],
+                        rhs=x_sb[:, b, s, a, 0 : BLOCK + ONES],
+                        start=(s == 0),
+                        stop=(s == SLICES - 1),
+                    )
 
             def tokens_first(t):
                 b, a = divmod(t, BANDS)
                 xt = tokens_first_pool.tile([P, SLICES, P], BF16, name="xt")
                 for s in range(SLICES):
-                    nc.tensor.transpose(xt[:, s, :], x_sb[:, b, s, BLOCK * a : BLOCK * (a + 1)], ident_bf[:])
+                    nc.tensor.transpose(xt[:, s, :], x_sb[:, b, s, a, 0:BLOCK], ident_bf[:])
                 xt_flat[t] = xt[:].rearrange("t s p -> t (s p)")
 
-            stats = {}
-            rstd = {}
-            assert E // BN_MAX == 2
-
-            def half_statistics(t, i):
-                if i == 0:
-                    stats[t] = small.tile([P, E // BN_MAX, 6], F32, name="stats")
-                nc.vector.bn_stats(out=stats[t][:, i, :], in_=xt_flat[t][:, BN_MAX * i : BN_MAX * (i + 1)])
-
             def deviation(t):
-                mean_var[t] = small.tile([P, 2], F32, name="mean_var")
-                nc.vector.bn_aggr(out=mean_var[t][:], in_=stats[t][:].rearrange("t i v -> t (i v)"))
-                std[t] = small.tile([P, 1], F32, name="std")
-                nc.scalar.activation(out=std[t][:], in_=mean_var[t][:, 1:2], func=ACT.Sqrt, bias=eps[:, 0:1], scale=1.0)
-
-            def inverse(t):
-                rstd[t] = small.tile([P, 1], F32, name="rstd")
-                nc.vector.reciprocal(out=rstd[t][:], in_=std[t][:])
-
-            def centre_and_scale(t):
-                offset = small.tile([P, 1], F32, name="offset")
+                diagonal = scratch.tile([P, BLOCK], F32, name="diagonal")
+                mean_square = small.tile([P, 1], F32, name="mean_square")
                 nc.vector.scalar_tensor_tensor(
-                    out=offset[:], in0=mean_var[t][:, 0:1], scalar=-1.0, in1=rstd[t][:], op0=ALU.mult, op1=ALU.mult
+                    out=diagonal[:], in0=sums_of[t][:, 0:BLOCK], scalar=1.0 / E, in1=ident_f[:],
+                    op0=ALU.mult, op1=ALU.mult, accum_out=mean_square[:],
                 )
+                neg_mean[t] = small.tile([P, 1], F32, name="neg_mean")
+                nc.vector.tensor_scalar(
+                    out=neg_mean[t][:], in0=sums_of[t][:, BLOCK : BLOCK + 1], scalar1=-1.0 / E, scalar2=None, op0=ALU.mult
+                )
+                neg_var = small.tile([P, 1], F32, name="neg_var")
+                nc.vector.scalar_tensor_tensor(
+                    out=neg_var[:], in0=neg_mean[t][:], scalar=neg_mean[t][:, 0:1], in1=mean_square[:],
+                    op0=ALU.mult, op1=ALU.subtract,
+                )
+                var = small.tile([P, 1], F32, name="var")
+                nc.vector.tensor_scalar(out=var[:], in0=neg_var[:], scalar1=0.0, scalar2=-1.0, op0=ALU.min, op1=ALU.mult)
+                std[t] = small.tile([P, 1], F32, name="std")
+                nc.scalar.activation(out=std[t][:], in_=var[:], func=ACT.Sqrt, bias=eps[:, 0:1], scale=1.0)
+
+            def centre_and_scale(t, on_scalar):
+                rstd = small.tile([P, 1], F32, name="rstd")
+                nc.vector.reciprocal(out=rstd[:], in_=std[t][:])
+                offset = small.tile([P, 1], F32, name="offset")
+                nc.vector.tensor_tensor(out=offset[:], in0=neg_mean[t][:], in1=rstd[:], op=ALU.mult)
                 z[t] = centred.tile([P, E], F32, name="z")
-                nc.scalar.activation(
-                    out=z[t][:], in_=xt_flat[t], func=ACT.Identity, bias=offset[:, 0:1], scale=rstd[t][:, 0:1]
-                )
+                if on_scalar:
+                    nc.scalar.activation(
+                        out=z[t][:], in_=xt_flat[t], func=ACT.Identity, bias=offset[:, 0:1], scale=rstd[:, 0:1]
+                    )
+                else:
+                    nc.vector.tensor_scalar(
+                        out=z[t][:], in0=xt_flat[t], scalar1=rstd[:, 0:1], scalar2=offset[:, 0:1],
+                        op0=ALU.mult, op1=ALU.add,
+                    )
 
             def channels_first_gain_shift(b, s, on_scalar):
                 zt = channels_first.tile([P, BANDS, P], F32, name="zt")
@@ -192,38 +217,10 @@ def tile_functatransformer_pa_kernel(
                     in_=normed[:, PACK * c : PACK * (c + 1), :, tokens_b].rearrange("p j l (u i) -> p l u j i", i=4),
                 )
 
-            for t in range(AHEAD):
-                tokens_first(t)
-            for t in range(all_bands + 2):
-                if t + AHEAD < all_bands:
-                    tokens_first(t + AHEAD)
-                if t < all_bands:
-                    half_statistics(t, 0)
-                if 1 <= t <= all_bands:
-                    deviation(t - 1)
-                if t == all_bands + 1:
-                    nc.vector.tensor_copy(out=shift[:], in_=shift_bf[:].rearrange("p c j -> p (c j)"))
-                if t >= 2:
-                    centre_and_scale(t - 2)
-                if t < all_bands:
-                    half_statistics(t, 1)
-                if t == all_bands:
-                    nc.vector.tensor_copy(out=gain[:], in_=gain_bf[:].rearrange("p c j -> p (c j)"))
-                if 1 <= t <= all_bands:
-                    inverse(t - 1)
-            for c in range(PASSES):
-                regroup_weights(0, c)
-            for c in range(PASSES):
-                quantise_weights(0, c)
-            for b in range(IMAGES):
-                for s in range(SLICES):
-                    channels_first_gain_shift(b, s, s % PACK != PACK - 2)
-                    if s % PACK == PACK - 1:
-                        group_words(b, s // PACK)
-
             per_call = QUANT // PACK
-            for i in range(IMAGES * TOKENS // per_call):
-                for c in range(PASSES):
+
+            def quantise_x(c, calls):
+                for i in calls:
                     nc.vector.quantize_mx(
                         out=x_codes[:, c, per_call * i : per_call * (i + 1)].bitcast(FP8X4),
                         scales=x_scales[:, c, per_call * i : per_call * (i + 1)],
@@ -231,6 +228,43 @@ def tile_functatransformer_pa_kernel(
                             "p l t j -> p (l t j)"
                         ),
                     )
+
+            on_vector = ((0, 0), (0, 1), (1, 3))
+
+            def back(b, s):
+                channels_first_gain_shift(b, s, (b, s) not in on_vector)
+                if s % PACK == PACK - 1:
+                    group_words(b, s // PACK)
+
+            first_chunk = [(regroup_weights, 0), (regroup_weights, 1), (quantise_weights, 0), (quantise_weights, 1)]
+            fill = {6: 1, 8: 2, 9: 1}
+            slices_back = 0
+            for t in range(AHEAD):
+                products_of_tokens(t)
+            for t in range(all_bands + 2):
+                if t + AHEAD < all_bands:
+                    products_of_tokens(t + AHEAD)
+                if t < all_bands:
+                    tokens_first(t)
+                    deviation(t)
+                if 1 <= t <= all_bands:
+                    centre_and_scale(t - 1, (t - 1) not in (0, all_bands - 1))
+                if t == 5:
+                    nc.vector.tensor_copy(out=gain[:], in_=gain_bf[:].rearrange("p c j -> p (c j)"))
+                    nc.vector.tensor_copy(out=shift[:], in_=shift_bf[:].rearrange("p c j -> p (c j)"))
+                for step, c in first_chunk[0 : fill.get(t, 0)]:
+                    step(0, c)
+                first_chunk = first_chunk[fill.get(t, 0) :]
+                if t >= 7:
+                    for s in range(slices_back, min(slices_back + 3, SLICES)):
+                        back(0, s)
+                    slices_back = min(slices_back + 3, SLICES)
+            for s in range(SLICES):
+                back(1, s)
+                if s == PACK - 1:
+                    quantise_x(0, (0, 1))
+            quantise_x(0, (2, 3))
+            quantise_x(1, (0, 1, 2, 3))
 
         with tc.tile_pool(name="stage", bufs=8, reuse_waits="tile") as stage, tc.tile_pool(
             name="stage_q", bufs=3, reuse_waits="tile"

@@ -82,20 +82,21 @@ def tile_functatransformer_pa_kernel(
         w_raw = {}
         grouped_w = {}
 
-        def regroup_weights(n, c):
+        def regroup_weights(n, c, lo=0, hi=N_TILE, on_vector=False):
             m, half = chunk_of[n]
-            grouped_w[(n, c)] = regroup.tile([P, N_TILE, PACK], BF16, name="grouped_w", align_bytes=64)
-            copy = nc.vector.tensor_copy if n == 0 else nc.scalar.copy
+            if lo == 0:
+                grouped_w[(n, c)] = regroup.tile([P, N_TILE, PACK], BF16, name="grouped_w", align_bytes=64)
+            copy = nc.vector.tensor_copy if on_vector else nc.scalar.copy
             copy(
-                out=grouped_w[(n, c)][:].rearrange("p (u i) j -> p u j i", i=4),
-                in_=w_raw[(m, c)][:, :, N_TILE * half : N_TILE * (half + 1)].rearrange("p j (u i) -> p u j i", i=4),
+                out=grouped_w[(n, c)][:, lo:hi, :].rearrange("p (u i) j -> p u j i", i=4),
+                in_=w_raw[(m, c)][:, :, N_TILE * half + lo : N_TILE * half + hi].rearrange("p j (u i) -> p u j i", i=4),
             )
 
-        def quantise_weights(n, c):
+        def quantise_weights(n, c, lo=0, hi=N_TILE):
             nc.vector.quantize_mx(
-                out=w_codes[:, c, N_TILE * n : N_TILE * (n + 1)].bitcast(FP8X4),
-                scales=w_scales[:, c, N_TILE * n : N_TILE * (n + 1)],
-                in_=grouped_w[(n, c)][:].rearrange("p n j -> p (n j)"),
+                out=w_codes[:, c, N_TILE * n + lo : N_TILE * n + hi].bitcast(FP8X4),
+                scales=w_scales[:, c, N_TILE * n + lo : N_TILE * n + hi],
+                in_=grouped_w[(n, c)][:, lo:hi, :].rearrange("p n j -> p (n j)"),
             )
 
         with tc.tile_pool(name="norm", bufs=1) as norm, tc.tile_pool(
@@ -236,8 +237,7 @@ def tile_functatransformer_pa_kernel(
                 if s % PACK == PACK - 1:
                     group_words(b, s // PACK)
 
-            first_chunk = [(regroup_weights, 0), (regroup_weights, 1), (quantise_weights, 0), (quantise_weights, 1)]
-            fill = {6: 1, 8: 2, 9: 1}
+            fill = (8, 9)
             slices_back = 0
             for t in range(AHEAD):
                 products_of_tokens(t)
@@ -252,9 +252,12 @@ def tile_functatransformer_pa_kernel(
                 if t == 5:
                     nc.vector.tensor_copy(out=gain[:], in_=gain_bf[:].rearrange("p c j -> p (c j)"))
                     nc.vector.tensor_copy(out=shift[:], in_=shift_bf[:].rearrange("p c j -> p (c j)"))
-                for step, c in first_chunk[0 : fill.get(t, 0)]:
-                    step(0, c)
-                first_chunk = first_chunk[fill.get(t, 0) :]
+                if t == fill[0]:
+                    for c in range(PASSES):
+                        regroup_weights(0, c, 0, N_MX, on_vector=True)
+                if t == fill[1]:
+                    for c in range(PASSES):
+                        quantise_weights(0, c, 0, N_MX)
                 if t >= 7:
                     for s in range(slices_back, min(slices_back + 3, SLICES)):
                         back(0, s)
@@ -265,6 +268,11 @@ def tile_functatransformer_pa_kernel(
                     quantise_x(0, (0, 1))
             quantise_x(0, (2, 3))
             quantise_x(1, (0, 1, 2, 3))
+            for lo, hi in ((N_MX, 2 * N_MX), (2 * N_MX, N_TILE)):
+                for c in range(PASSES):
+                    regroup_weights(0, c, lo, hi)
+            for c in range(PASSES):
+                quantise_weights(0, c, N_MX, 2 * N_MX)
 
         with tc.tile_pool(name="stage", bufs=8, reuse_waits="tile") as stage, tc.tile_pool(
             name="stage_q", bufs=3, reuse_waits="tile"
@@ -323,7 +331,10 @@ def tile_functatransformer_pa_kernel(
                                 .to_broadcast([P, heads_mx, l_bank, HEAD]),
                                 op=ALU.add,
                             )
-                        if q == 0 and k < PASSES and n + 1 < all_chunks:
+                        if (n, q, k) == (0, 0, 1):
+                            for c in range(PASSES):
+                                quantise_weights(0, c, 2 * N_MX, N_TILE)
+                        if q == (2 if n == 0 else 0) and k < PASSES and n + 1 < all_chunks:
                             quantise_weights(n + 1, k)
                     for h in range(heads_mx):
                         nc.sync.dma_start(

@@ -56,6 +56,9 @@ def tile_functatransformer_pa_kernel(
     with tc.manual_schedule(), tc.tile_pool(name="keep", bufs=1) as keep, tc.tile_pool(
         name="regroup", bufs=4
     ) as regroup:
+        x_sb = keep.tile([P, IMAGES, SLICES, BANDS, BLOCK + PAD], BF16)
+        nc.vector.memset(x_sb[:, :, :, :, BLOCK : BLOCK + PAD].rearrange("p b s a k -> p (b s a) k"), 1.0)
+
         ident_bf = keep.tile([P, P], BF16)
         make_identity(nc, ident_bf[:])
         ident_f = keep.tile([P, P], F32)
@@ -106,8 +109,6 @@ def tile_functatransformer_pa_kernel(
         ) as scratch, tc.psum_pool(name="moments", bufs=2) as moments_pool, tc.psum_pool(
             name="tokens_first", bufs=3
         ) as tokens_first_pool, tc.psum_pool(name="channels_first", bufs=3) as channels_first:
-            x_sb = norm.tile([P, IMAGES, SLICES, BANDS, BLOCK + PAD], BF16)
-            nc.vector.memset(x_sb[:, :, :, :, BLOCK : BLOCK + PAD].rearrange("p b s a k -> p (b s a) k"), 1.0)
             first = SHIFT * COLS
             for b in range(IMAGES):
                 for a in range(BANDS):
@@ -230,7 +231,7 @@ def tile_functatransformer_pa_kernel(
                         ),
                     )
 
-            on_vector = ((0, 0), (0, 1), (1, 3))
+            on_vector = ((0, 2), (1, 2), (1, 7))
 
             def back(b, s):
                 channels_first_gain_shift(b, s, (b, s) not in on_vector)
@@ -248,8 +249,8 @@ def tile_functatransformer_pa_kernel(
                     tokens_first(t)
                     deviation(t)
                 if 1 <= t <= all_bands:
-                    centre_and_scale(t - 1, (t - 1) not in (0, all_bands - 1))
-                if t == 5:
+                    centre_and_scale(t - 1, t - 1 < all_bands - 2)
+                if t == 6:
                     nc.vector.tensor_copy(out=gain[:], in_=gain_bf[:].rearrange("p c j -> p (c j)"))
                     nc.vector.tensor_copy(out=shift[:], in_=shift_bf[:].rearrange("p c j -> p (c j)"))
                 if t == fill[0]:

@@ -56,8 +56,9 @@ def tile_functatransformer_pa_kernel(
     with tc.manual_schedule(), tc.tile_pool(name="keep", bufs=1) as keep, tc.tile_pool(
         name="regroup", bufs=4
     ) as regroup:
-        x_sb = keep.tile([P, IMAGES, SLICES, BANDS, BLOCK + PAD], BF16)
-        nc.vector.memset(x_sb[:, :, :, :, BLOCK : BLOCK + PAD].rearrange("p b s a k -> p (b s a) k"), 1.0)
+        x_sb = keep.tile([P, IMAGES, SLICES, BANDS // 2, PAD + 2 * BLOCK + PAD], BF16)
+        for lo in (0, PAD + 2 * BLOCK):
+            nc.vector.memset(x_sb[:, :, :, :, lo : lo + PAD].rearrange("p b s a k -> p (b s a) k"), 1.0)
 
         ident_bf = keep.tile([P, P], BF16)
         make_identity(nc, ident_bf[:])
@@ -111,15 +112,23 @@ def tile_functatransformer_pa_kernel(
         ) as tokens_first_pool, tc.psum_pool(name="channels_first", bufs=3) as channels_first:
             first = SHIFT * COLS
             for b in range(IMAGES):
-                for a in range(BANDS):
-                    start = BLOCK * a + first
-                    whole = min(BLOCK, TOKENS - start)
+                for i in range(BANDS // 2):
+                    start = 2 * BLOCK * i + first
+                    whole = min(2 * BLOCK, TOKENS - start)
                     for c in range(PASSES):
                         source = x[b, K_PASS * c : K_PASS * (c + 1)].rearrange("(p j) r k -> p j (r k)", j=PACK)
                         slices_c = slice(PACK * c, PACK * (c + 1))
-                        nc.sync.dma_start(out=x_sb[:, b, slices_c, a, 0:whole], in_=source[:, :, start : start + whole])
-                        if whole < BLOCK:
-                            nc.sync.dma_start(out=x_sb[:, b, slices_c, a, whole:BLOCK], in_=source[:, :, 0 : BLOCK - whole])
+                        nc.sync.dma_start(
+                            out=x_sb[:, b, slices_c, i, PAD : PAD + whole], in_=source[:, :, start : start + whole]
+                        )
+                    if whole < 2 * BLOCK:
+                        for c in range(PASSES):
+                            source = x[b, K_PASS * c : K_PASS * (c + 1)].rearrange("(p j) r k -> p j (r k)", j=PACK)
+                            slices_c = slice(PACK * c, PACK * (c + 1))
+                            nc.sync.dma_start(
+                                out=x_sb[:, b, slices_c, i, PAD + whole : PAD + 2 * BLOCK],
+                                in_=source[:, :, 0 : 2 * BLOCK - whole],
+                            )
             with nc.allow_non_contiguous_dma(reason="two small vectors, 4 channels to a partition"):
                 nc.sync.dma_start(out=gain_bf[:], in_=ln1_g.rearrange("(c p j) -> p c j", c=PASSES, j=PACK))
                 nc.sync.dma_start(out=shift_bf[:], in_=ln1_b.rearrange("(c p j) -> p c j", c=PASSES, j=PACK))
@@ -142,12 +151,14 @@ def tile_functatransformer_pa_kernel(
 
             def products_of_tokens(t):
                 b, a = divmod(t, BANDS)
+                lo = PAD + BLOCK * (a % 2)
+                before = ONES * (1 - a % 2)
                 sums_of[t] = moments_pool.tile([P, BLOCK + ONES], F32, name="sums_of")
                 for s in range(SLICES):
                     nc.tensor.matmul(
                         out=sums_of[t][:],
-                        lhsT=x_sb[:, b, s, a, 0:BLOCK],
-                        rhs=x_sb[:, b, s, a, 0 : BLOCK + ONES],
+                        lhsT=x_sb[:, b, s, a // 2, lo : lo + BLOCK],
+                        rhs=x_sb[:, b, s, a // 2, lo - before : lo - before + BLOCK + ONES],
                         start=(s == 0),
                         stop=(s == SLICES - 1),
                     )
@@ -156,19 +167,22 @@ def tile_functatransformer_pa_kernel(
                 b, a = divmod(t, BANDS)
                 xt = tokens_first_pool.tile([P, SLICES, P], BF16, name="xt")
                 for s in range(SLICES):
-                    nc.tensor.transpose(xt[:, s, :], x_sb[:, b, s, a, 0:BLOCK], ident_bf[:])
+                    lo = PAD + BLOCK * (a % 2)
+                    nc.tensor.transpose(xt[:, s, :], x_sb[:, b, s, a // 2, lo : lo + BLOCK], ident_bf[:])
                 xt_flat[t] = xt[:].rearrange("t s p -> t (s p)")
 
             def deviation(t):
+                square = ONES * (1 - t % 2)
+                total = BLOCK * (t % 2)
                 diagonal = scratch.tile([P, BLOCK], F32, name="diagonal")
                 mean_square = small.tile([P, 1], F32, name="mean_square")
                 nc.vector.scalar_tensor_tensor(
-                    out=diagonal[:], in0=sums_of[t][:, 0:BLOCK], scalar=1.0 / E, in1=ident_f[:],
+                    out=diagonal[:], in0=sums_of[t][:, square : square + BLOCK], scalar=1.0 / E, in1=ident_f[:],
                     op0=ALU.mult, op1=ALU.mult, accum_out=mean_square[:],
                 )
                 neg_mean[t] = small.tile([P, 1], F32, name="neg_mean")
                 nc.vector.tensor_scalar(
-                    out=neg_mean[t][:], in0=sums_of[t][:, BLOCK : BLOCK + 1], scalar1=-1.0 / E, scalar2=None, op0=ALU.mult
+                    out=neg_mean[t][:], in0=sums_of[t][:, total : total + 1], scalar1=-1.0 / E, scalar2=None, op0=ALU.mult
                 )
                 neg_var = small.tile([P, 1], F32, name="neg_var")
                 nc.vector.scalar_tensor_tensor(

@@ -189,14 +189,13 @@ def tile_functatransformer_pa_kernel(
                     out=neg_var[:], in0=neg_mean[t][:], scalar=neg_mean[t][:, 0:1], in1=mean_square[:],
                     op0=ALU.mult, op1=ALU.subtract,
                 )
-                var = small.tile([P, 1], F32, name="var")
-                nc.vector.tensor_scalar(out=var[:], in0=neg_var[:], scalar1=0.0, scalar2=-1.0, op0=ALU.min, op1=ALU.mult)
                 std[t] = small.tile([P, 1], F32, name="std")
-                nc.scalar.activation(out=std[t][:], in_=var[:], func=ACT.Sqrt, bias=eps[:, 0:1], scale=1.0)
+                nc.scalar.activation(
+                    out=std[t][:], in_=neg_var[:], func=ACT.Abs_reciprocal_sqrt, bias=eps[:, 0:1], scale=-1.0
+                )
 
             def centre_and_scale(t, on_scalar):
-                rstd = small.tile([P, 1], F32, name="rstd")
-                nc.vector.reciprocal(out=rstd[:], in_=std[t][:])
+                rstd = std[t]
                 offset = small.tile([P, 1], F32, name="offset")
                 nc.vector.tensor_tensor(out=offset[:], in0=neg_mean[t][:], in1=rstd[:], op=ALU.mult)
                 z[t] = centred.tile([P, E], F32, name="z")

from concourse.masks import make_identity
import concourse.mybir as mybir

BF16 = mybir.dt.bfloat16
F32 = mybir.dt.float32
U32 = mybir.dt.uint32
U8 = mybir.dt.uint8
FP8X4 = mybir.dt.float8_e4m3fn_x4
ACT = mybir.ActivationFunctionType
ALU = mybir.AluOpType

P = 128
PACK = 4
K_PASS = P * PACK
IMAGES = 2
E = 1024
ROWS, COLS = 32, 16
TOKENS = ROWS * COLS
WIN = 8
SHIFT = WIN // 2
HEAD = 32
EPS = 1e-5
PASSES = E // K_PASS
SLICES = PASSES * PACK
BLOCK = WIN * COLS
BANDS = ROWS // WIN
RUN = (COLS // WIN) * WIN
N_TILE = 512
HEADS_TILE = N_TILE // HEAD
CHUNKS = E // N_TILE
N_MX = 128
N_MX_Q = 256
FACTOR = HEAD**-0.5
HEADS_MX = N_MX // HEAD
L_BANK = N_TILE // N_MX
assert WIN // L_BANK == PASSES
PAD = 16
ONES = 2
AHEAD = 2
QUANT = 1024

FLOPS = 2 * IMAGES * TOKENS * E * 3 * E


def tile_functatransformer_pa_kernel(
    tc, x, ln1_g, ln1_b, Wq, bq, Wk, bk, Wv, bv, out_0, out_1, out_2
):
    nc = tc.nc
    weights = [Wq, Wk, Wv]
    biases = [bq, bk, bv]
    outs = [out_0, out_1, out_2]
    all_bands = IMAGES * BANDS
    chunk_of = [(1, 0), (1, 1), (2, 0), (0, 0), (0, 1), (2, 1)]
    all_chunks = len(chunk_of)

    with tc.manual_schedule(), tc.tile_pool(name="keep", bufs=1) as keep, tc.tile_pool(
        name="regroup", bufs=4
    ) as regroup:
        x_sb = keep.tile([P, IMAGES, SLICES, BANDS // 2, PAD + 2 * BLOCK + PAD], BF16)
        for lo in (0, PAD + 2 * BLOCK):
            nc.vector.memset(x_sb[:, :, :, :, lo : lo + PAD].rearrange("p b s a k -> p (b s a) k"), 1.0)

        ident_bf = keep.tile([P, P], BF16)
        make_identity(nc, ident_bf[:])
        ident_f = keep.tile([P, P], F32)
        make_identity(nc, ident_f[:])
        to_window = keep.tile([P, P], F32)
        by_image = ident_f[:].rearrange("p (r g l) -> p l g r", r=WIN, g=2, l=WIN)
        by_window = to_window[:].rearrange("p (l g r) -> p l g r", l=WIN, g=2, r=WIN)
        nc.vector.tensor_copy(out=by_window[:, 0:SHIFT, :, :], in_=by_image[:, SHIFT:WIN, :, :])
        for g in range(2):
            nc.vector.tensor_copy(out=by_window[:, SHIFT:WIN, g, :], in_=by_image[:, 0:SHIFT, 1 - g, :])
        eps = keep.tile([P, 1], F32)
        nc.vector.memset(eps[:], EPS)

        x_codes = keep.tile([P, PASSES, IMAGES * TOKENS], U32, align_bytes=64)
        x_scales = keep.tile([P, PASSES, IMAGES * TOKENS], U8, align_bytes=64)
        w_codes = keep.tile([P, PASSES, 3 * E], U32, align_bytes=64)
        w_scales = keep.tile([P, PASSES, 3 * E], U8, align_bytes=64)
        bias_bf = keep.tile([P, 3, E], BF16)
        bias_q = keep.tile([P, E], F32)
        gain_bf = keep.tile([P, PASSES, PACK], BF16)
        shift_bf = keep.tile([P, PASSES, PACK], BF16)
        gain = keep.tile([P, SLICES], F32)
        shift = keep.tile([P, SLICES], F32)
        w_raw = {}
        grouped_w = {}

        def regroup_weights(n, c, lo=0, hi=N_TILE, on_vector=False):
            m, half = chunk_of[n]
            if lo == 0:
                grouped_w[(n, c)] = regroup.tile([P, N_TILE, PACK], BF16, name="grouped_w", align_bytes=64)
            copy = nc.vector.tensor_copy if on_vector else nc.scalar.copy
            copy(
                out=grouped_w[(n, c)][:, lo:hi, :].rearrange("p (u i) j -> p u j i", i=4),
                in_=w_raw[(m, c)][:, :, N_TILE * half + lo : N_TILE * half + hi].rearrange("p j (u i) -> p u j i", i=4),
            )

        def quantise_weights(n, c, lo=0, hi=N_TILE):
            nc.vector.quantize_mx(
                out=w_codes[:, c, N_TILE * n + lo : N_TILE * n + hi].bitcast(FP8X4),
                scales=w_scales[:, c, N_TILE * n + lo : N_TILE * n + hi],
                in_=grouped_w[(n, c)][:, lo:hi, :].rearrange("p n j -> p (n j)"),
            )

        with tc.tile_pool(name="norm", bufs=1) as norm, tc.tile_pool(
            name="centred", bufs=all_bands
        ) as centred, tc.tile_pool(name="small", bufs=all_bands) as small, tc.tile_pool(
            name="scratch", bufs=2
        ) as scratch, tc.psum_pool(name="moments", bufs=2) as moments_pool, tc.psum_pool(
            name="tokens_first", bufs=3
        ) as tokens_first_pool, tc.psum_pool(name="channels_first", bufs=3) as channels_first:
            first = SHIFT * COLS
            for b in range(IMAGES):
                for i in range(BANDS // 2):
                    start = 2 * BLOCK * i + first
                    whole = min(2 * BLOCK, TOKENS - start)
                    for c in range(PASSES):
                        source = x[b, K_PASS * c : K_PASS * (c + 1)].rearrange("(p j) r k -> p j (r k)", j=PACK)
                        slices_c = slice(PACK * c, PACK * (c + 1))
                        nc.sync.dma_start(
                            out=x_sb[:, b, slices_c, i, PAD : PAD + whole], in_=source[:, :, start : start + whole]
                        )
                    if whole < 2 * BLOCK:
                        for c in range(PASSES):
                            source = x[b, K_PASS * c : K_PASS * (c + 1)].rearrange("(p j) r k -> p j (r k)", j=PACK)
                            slices_c = slice(PACK * c, PACK * (c + 1))
                            nc.sync.dma_start(
                                out=x_sb[:, b, slices_c, i, PAD + whole : PAD + 2 * BLOCK],
                                in_=source[:, :, 0 : 2 * BLOCK - whole],
                            )
            with nc.allow_non_contiguous_dma(reason="two small vectors, 4 channels to a partition"):
                nc.sync.dma_start(out=gain_bf[:], in_=ln1_g.rearrange("(c p j) -> p c j", c=PASSES, j=PACK))
                nc.sync.dma_start(out=shift_bf[:], in_=ln1_b.rearrange("(c p j) -> p c j", c=PASSES, j=PACK))
            for m in (1, 2, 0):
                for c in range(PASSES):
                    w_raw[(m, c)] = keep.tile([P, PACK, E], BF16, name="w_raw_%d_%d" % (m, c))
                    nc.sync.dma_start(
                        out=w_raw[(m, c)][:],
                        in_=weights[m][K_PASS * c : K_PASS * (c + 1), :].rearrange("(p j) n -> p j n", j=PACK),
                    )
                nc.sync.dma_start(out=bias_bf[:, m, :], in_=biases[m].partition_broadcast(P))

            normed = norm.tile([P, SLICES, WIN, all_bands * RUN], BF16)
            grouped_x = norm.tile([P, PASSES, WIN, all_bands * RUN, PACK], BF16, align_bytes=64)
            sums_of = {}
            xt_flat = {}
            neg_mean = {}
            std = {}
            z = {}

            def products_of_tokens(t):
                b, a = divmod(t, BANDS)
                lo = PAD + BLOCK * (a % 2)
                before = ONES * (1 - a % 2)
                sums_of[t] = moments_pool.tile([P, BLOCK + ONES], F32, name="sums_of")
                for s in range(SLICES):
                    nc.tensor.matmul(
                        out=sums_of[t][:],
                        lhsT=x_sb[:, b, s, a // 2, lo : lo + BLOCK],
                        rhs=x_sb[:, b, s, a // 2, lo - before : lo - before + BLOCK + ONES],
                        start=(s == 0),
                        stop=(s == SLICES - 1),
                    )

            def tokens_first(t):
                b, a = divmod(t, BANDS)
                xt = tokens_first_pool.tile([P, SLICES, P], BF16, name="xt")
                for s in range(SLICES):
                    lo = PAD + BLOCK * (a % 2)
                    nc.tensor.transpose(xt[:, s, :], x_sb[:, b, s, a // 2, lo : lo + BLOCK], ident_bf[:])
                xt_flat[t] = xt[:].rearrange("t s p -> t (s p)")

            def deviation(t):
                square = ONES * (1 - t % 2)
                total = BLOCK * (t % 2)
                diagonal = scratch.tile([P, BLOCK], F32, name="diagonal")
                mean_square = small.tile([P, 1], F32, name="mean_square")
                nc.vector.scalar_tensor_tensor(
                    out=diagonal[:], in0=sums_of[t][:, square : square + BLOCK], scalar=1.0 / E, in1=ident_f[:],
                    op0=ALU.mult, op1=ALU.mult, accum_out=mean_square[:],
                )
                neg_mean[t] = small.tile([P, 1], F32, name="neg_mean")
                nc.vector.tensor_scalar(
                    out=neg_mean[t][:], in0=sums_of[t][:, total : total + 1], scalar1=-1.0 / E, scalar2=None, op0=ALU.mult
                )
                neg_var = small.tile([P, 1], F32, name="neg_var")
                nc.vector.scalar_tensor_tensor(
                    out=neg_var[:], in0=neg_mean[t][:], scalar=neg_mean[t][:, 0:1], in1=mean_square[:],
                    op0=ALU.mult, op1=ALU.subtract,
                )
                std[t] = small.tile([P, 1], F32, name="std")
                nc.scalar.activation(
                    out=std[t][:], in_=neg_var[:], func=ACT.Abs_reciprocal_sqrt, bias=eps[:, 0:1], scale=-1.0
                )

            def centre_and_scale(t, on_scalar):
                rstd = std[t]
                offset = small.tile([P, 1], F32, name="offset")
                nc.vector.tensor_tensor(out=offset[:], in0=neg_mean[t][:], in1=rstd[:], op=ALU.mult)
                z[t] = centred.tile([P, E], F32, name="z")
                if on_scalar:
                    nc.scalar.activation(
                        out=z[t][:], in_=xt_flat[t], func=ACT.Identity, bias=offset[:, 0:1], scale=rstd[:, 0:1]
                    )
                else:
                    nc.vector.tensor_scalar(
                        out=z[t][:], in0=xt_flat[t], scalar1=rstd[:, 0:1], scalar2=offset[:, 0:1],
                        op0=ALU.mult, op1=ALU.add,
                    )

            def channels_first_gain_shift(b, s, on_scalar):
                zt = channels_first.tile([P, BANDS, P], F32, name="zt")
                for a in range(BANDS):
                    nc.tensor.transpose(zt[:, a, :], z[BANDS * b + a][:, P * s : P * (s + 1)], to_window[:])
                zt_by_l = zt[:].rearrange("p a (l t) -> p l a t", l=WIN)
                normed_s = normed[:, s, :, BANDS * RUN * b : BANDS * RUN * (b + 1)].rearrange("p l (a t) -> p l a t", a=BANDS)
                if on_scalar:
                    nc.scalar.activation(
                        out=normed_s, in_=zt_by_l, func=ACT.Identity, bias=shift[:, s : s + 1], scale=gain[:, s : s + 1]
                    )
                else:
                    nc.vector.tensor_scalar(
                        out=normed_s, in0=zt_by_l, scalar1=gain[:, s : s + 1], scalar2=shift[:, s : s + 1],
                        op0=ALU.mult, op1=ALU.add,
                    )

            def group_words(b, c):
                tokens_b = slice(BANDS * RUN * b, BANDS * RUN * (b + 1))
                nc.vector.tensor_copy(
                    out=grouped_x[:, c, :, tokens_b, :].rearrange("p l (u i) j -> p l u j i", i=4),
                    in_=normed[:, PACK * c : PACK * (c + 1), :, tokens_b].rearrange("p j l (u i) -> p l u j i", i=4),
                )

            per_call = QUANT // PACK

            def quantise_x(c, calls):
                for i in calls:
                    nc.vector.quantize_mx(
                        out=x_codes[:, c, per_call * i : per_call * (i + 1)].bitcast(FP8X4),
                        scales=x_scales[:, c, per_call * i : per_call * (i + 1)],
                        in_=grouped_x[:, c, (per_call // P) * i : (per_call // P) * (i + 1), :, :].rearrange(
                            "p l t j -> p (l t j)"
                        ),
                    )

            on_vector = ((0, 2), (1, 2), (1, 7))

            def back(b, s):
                channels_first_gain_shift(b, s, (b, s) not in on_vector)
                if s % PACK == PACK - 1:
                    group_words(b, s // PACK)

            fill = (8, 9)
            slices_back = 0
            for t in range(AHEAD):
                products_of_tokens(t)
            for t in range(all_bands + 2):
                if t + AHEAD < all_bands:
                    products_of_tokens(t + AHEAD)
                if t < all_bands:
                    tokens_first(t)
                    deviation(t)
                if 1 <= t <= all_bands:
                    centre_and_scale(t - 1, t - 1 < all_bands - 2)
                if t == 6:
                    nc.vector.tensor_copy(out=gain[:], in_=gain_bf[:].rearrange("p c j -> p (c j)"))
                    nc.vector.tensor_copy(out=shift[:], in_=shift_bf[:].rearrange("p c j -> p (c j)"))
                if t == fill[0]:
                    for c in range(PASSES):
                        regroup_weights(0, c, 0, N_MX, on_vector=True)
                if t == fill[1]:
                    for c in range(PASSES):
                        quantise_weights(0, c, 0, N_MX)
                if t >= 7:
                    for s in range(slices_back, min(slices_back + 3, SLICES)):
                        back(0, s)
                    slices_back = min(slices_back + 3, SLICES)
            for s in range(SLICES):
                back(1, s)
                if s == PACK - 1:
                    quantise_x(0, (0, 1))
            quantise_x(0, (2, 3))
            quantise_x(1, (0, 1, 2, 3))
            for lo, hi in ((N_MX, 2 * N_MX), (2 * N_MX, N_TILE)):
                for c in range(PASSES):
                    regroup_weights(0, c, lo, hi)
            for c in range(PASSES):
                quantise_weights(0, c, N_MX, 2 * N_MX)

        with tc.tile_pool(name="stage", bufs=8, reuse_waits="tile") as stage, tc.tile_pool(
            name="stage_q", bufs=3, reuse_waits="tile"
        ) as stage_q, tc.psum_pool(name="sums", bufs=8, reuse_waits="tile") as sums:
            for c in range(PASSES):
                regroup_weights(1, c)
            for n in range(all_chunks):
                m, half = chunk_of[n]
                by_head = outs[m].rearrange("b w h (r l) d -> h (b w) r (l d)", r=WIN)
                if n + 2 < all_chunks:
                    for c in range(PASSES):
                        regroup_weights(n + 2, c)
                    if chunk_of[n + 2] == (0, 0):
                        nc.scalar.activation(out=bias_q[:], in_=bias_bf[:, 0, :], func=ACT.Copy, scale=FACTOR)
                n_mx = N_MX_Q if m == 0 else N_MX
                heads_mx = n_mx // HEAD
                l_bank = N_TILE // n_mx
                for q in range(N_TILE // n_mx):
                    w_cols = slice(N_TILE * n + n_mx * q, N_TILE * n + n_mx * (q + 1))
                    bias_cols = slice(N_TILE * half + n_mx * q, N_TILE * half + n_mx * (q + 1))
                    if m == 0:
                        staged = stage_q.tile([P, heads_mx, WIN, HEAD], F32, name="staged_q")
                    else:
                        staged = stage.tile([P, heads_mx, WIN, HEAD], F32, name="staged")
                    for k in range(WIN // l_bank):
                        acc = sums.tile([P, l_bank, n_mx], F32, name="acc")
                        for i in range(l_bank):
                            tokens_l = slice(P * (l_bank * k + i), P * (l_bank * k + i + 1))
                            for c in range(PASSES):
                                nc.tensor.matmul_mx(
                                    out=acc[:, i, :],
                                    lhsT=x_codes[:, c, tokens_l].bitcast(FP8X4),
                                    lhsT_scale=x_scales[:, c, tokens_l],
                                    rhs=w_codes[:, c, w_cols].bitcast(FP8X4),
                                    rhs_scale=w_scales[:, c, w_cols],
                                    start=(c == 0),
                                    stop=(c == PASSES - 1),
                                )
                        if m == 0:
                            for i in range(l_bank):
                                nc.vector.scalar_tensor_tensor(
                                    out=staged[:, :, l_bank * k + i, :],
                                    in0=acc[:, i, :].rearrange("p (h d) -> p h d", d=HEAD),
                                    scalar=FACTOR,
                                    in1=bias_q[:, bias_cols].rearrange("p (h d) -> p h d", d=HEAD),
                                    op0=ALU.mult,
                                    op1=ALU.add,
                                )
                        else:
                            nc.vector.tensor_tensor(
                                out=staged[:, :, l_bank * k : l_bank * (k + 1), :],
                                in0=acc[:].rearrange("p i (h d) -> p h i d", d=HEAD),
                                in1=bias_bf[:, m, bias_cols]
                                .rearrange("p (h d) -> p h d", d=HEAD)
                                .unsqueeze(2)
                                .to_broadcast([P, heads_mx, l_bank, HEAD]),
                                op=ALU.add,
                            )
                        if (n, q, k) == (0, 0, 1):
                            for c in range(PASSES):
                                quantise_weights(0, c, 2 * N_MX, N_TILE)
                        if q == (2 if n == 0 else 0) and k < PASSES and n + 1 < all_chunks:
                            quantise_weights(n + 1, k)
                    for h in range(heads_mx):
                        nc.sync.dma_start(
                            out=by_head[HEADS_TILE * half + heads_mx * q + h],
                            in_=staged[:, h, :, :].rearrange("p l d -> p (l d)"),
                        )
